import numpy as np
import ml_dtypes


def mxq(x, axis, fmt="e4m3"):
    dtype, down = {"e4m3": (ml_dtypes.float8_e4m3fn, 7), "e5m2": (ml_dtypes.float8_e5m2, 14)}[fmt]
    v = np.moveaxis(np.asarray(x, np.float32).astype(ml_dtypes.bfloat16).astype(np.float64), axis, -1)
    blocks = v.reshape(v.shape[:-1] + (-1, 32))
    amax = np.abs(blocks).max(-1, keepdims=True)
    byte = np.maximum(np.where(amax > 0, np.frexp(amax)[1] - 1 + 127, 0) - down, 1)
    scale = np.exp2(byte - 127.0)
    codes = (blocks / scale).astype(np.float32).astype(dtype).astype(np.float64)
    return np.moveaxis((codes * scale).reshape(v.shape), -1, axis)


WIDE = False


def mx_kscale(k):
    if not WIDE:
        return np.ones(k)
    levels = np.array([10, -10, 5, -5, 0])
    a = np.random.permutation(np.resize(levels, k // 512 * 4)).reshape(k // 512, 4)
    idx = np.arange(k)
    return np.exp2(a[idx // 512, idx % 128 // 32])


BF16 = ml_dtypes.bfloat16


def bf(x):
    return np.asarray(x, np.float32).astype(BF16)


def f64(x):
    return np.asarray(x).astype(np.float64)


B, D, DO, H, T, P = 128, 1024, 1024, 256, 8, 2


def setup_inputs():
    s = mx_kscale(D)
    return {"transformed": bf(np.random.standard_normal((B, D)) * 1.2 * s),
            "coeff": bf(np.random.standard_normal((B, P)) * 0.45),
            "task_mats": bf(np.random.standard_normal((P, D, D)) / np.sqrt(D) / s[None, :, None] * s[None, None, :])}


def reference(transformed, coeff, task_mats):
    x, c, m = f64(transformed), f64(coeff), f64(task_mats)
    for j in range(P):
        x = x + c[:, j:j + 1] * (mxq(x, 1, "e4m3") @ mxq(m[j], 0, "e4m3"))
    return x

@@ -1,0 +1,170 @@
+from contextlib import ExitStack
+
+import concourse.mybir as mybir
+from concourse.masks import make_identity
+
+F32 = mybir.dt.float32
+BF16 = mybir.dt.bfloat16
+U32 = mybir.dt.uint32
+U8 = mybir.dt.uint8
+FP8X4 = mybir.dt.float8_e4m3fn_x4
+MULT = mybir.AluOpType.mult
+ADD = mybir.AluOpType.add
+
+P = 128
+PACK = 4
+K_PASS = P * PACK
+D = 1024
+STEPS = 2
+PASSES = D // K_PASS
+HALF = 512
+HALVES = D // HALF
+RUN = 4
+
+SCALAR_COLS = 288
+
+FLOPS = 2 * STEPS * P * D * D
+
+
+def tile_precomputedmetanet_pa_s_kernel(tc, transformed, coeff, task_mats, out):
+    nc = tc.nc
+    with ExitStack() as ctx:
+        keep = ctx.enter_context(tc.tile_pool(name="keep", bufs=1))
+        stage = ctx.enter_context(tc.tile_pool(name="stage", bufs=3))
+        psum = ctx.enter_context(tc.psum_pool(name="psum", bufs=1))
+
+        x_sb = keep.tile([P, D], BF16)
+        nc.scalar.dma_start(out=x_sb[:], in_=transformed)
+        coeff_bf = keep.tile([P, STEPS], BF16)
+        nc.scalar.dma_start(out=coeff_bf[:], in_=coeff)
+
+        raw = [
+            [keep.tile([P, PACK, D], BF16, name="raw_%d_%d" % (j, g)) for g in range(PASSES)]
+            for j in range(STEPS)
+        ]
+        by_k = task_mats.rearrange("j (g u p e) n -> j g p u e n", g=PASSES, u=2, p=P, e=2)
+        for h in range(HALVES):
+            for u in range(2):
+                nc.sync.dma_start(
+                    out=raw[0][0][:, 2 * u : 2 * u + 2, h * HALF : (h + 1) * HALF],
+                    in_=by_k[0, 0, :, u, :, h * HALF : (h + 1) * HALF],
+                )
+        for j in range(STEPS):
+            for g in range(PASSES):
+                if (j, g) != (0, 0):
+                    nc.sync.dma_start(
+                        out=raw[j][g][:].rearrange("p (u e) n -> p u e n", u=2),
+                        in_=by_k[j, g],
+                    )
+
+        ident = keep.tile([P, P], F32)
+        make_identity(nc, ident[:])
+        coeff_f32 = keep.tile([P, STEPS], F32)
+        nc.vector.tensor_copy(out=coeff_f32[:], in_=coeff_bf[:])
+
+        m_codes = [
+            [keep.tile([P, D], U32, align_bytes=64, name="m_codes_%d_%d" % (j, g)) for g in range(PASSES)]
+            for j in range(STEPS)
+        ]
+        m_scales = [
+            [keep.tile([P, D], U8, align_bytes=64, name="m_scales_%d_%d" % (j, g)) for g in range(PASSES)]
+            for j in range(STEPS)
+        ]
+        f_grouped = [keep.tile([P, PASSES * P * PACK], BF16, align_bytes=64, name="f_grouped_%d" % j) for j in range(STEPS)]
+        f_codes = [keep.tile([P, PASSES * P], U32, align_bytes=64, name="f_codes_%d" % j) for j in range(STEPS)]
+        f_scales = [keep.tile([P, PASSES * P], U8, align_bytes=64, name="f_scales_%d" % j) for j in range(STEPS)]
+
+        x1 = keep.tile([P, D], F32)
+        result = keep.tile([P, D], F32)
+        y = [
+            [psum.tile([P, HALF], F32, name="y_%d_%d" % (j, h)) for h in range(HALVES)]
+            for j in range(STEPS)
+        ]
+
+        def regroup(j, g, h):
+            grouped = stage.tile([P, HALF, PACK], BF16, align_bytes=64)
+            first = h * HALF
+            nc.scalar.copy(
+                out=grouped[:, :SCALAR_COLS, :].rearrange("p (c i) t -> p c t i", i=RUN),
+                in_=raw[j][g][:, :, first : first + SCALAR_COLS].rearrange("p t (c i) -> p c t i", i=RUN),
+            )
+            nc.vector.tensor_copy(
+                out=grouped[:, SCALAR_COLS:, :].rearrange("p (c i) t -> p c t i", i=RUN),
+                in_=raw[j][g][:, :, first + SCALAR_COLS : first + HALF].rearrange("p t (c i) -> p c t i", i=RUN),
+            )
+            return grouped
+
+        def quantise_and_multiply(j, g, h, grouped):
+            cols = slice(h * HALF, (h + 1) * HALF)
+            samples = slice(g * P, (g + 1) * P)
+            nc.vector.quantize_mx(
+                out=m_codes[j][g][:, cols].bitcast(FP8X4),
+                scales=m_scales[j][g][:, cols],
+                in_=grouped[:].rearrange("p c t -> p (c t)"),
+            )
+            nc.tensor.matmul_mx(
+                out=y[j][h][:],
+                lhsT=f_codes[j][:, samples].bitcast(FP8X4),
+                lhsT_scale=f_scales[j][:, samples],
+                rhs=m_codes[j][g][:, cols].bitcast(FP8X4),
+                rhs_scale=m_scales[j][g][:, cols],
+                start=(g == 0),
+                stop=(g == PASSES - 1),
+            )
+
+        def quantise_features(j, first_pass, end_pass):
+            nc.vector.quantize_mx(
+                out=f_codes[j][:, first_pass * P : end_pass * P].bitcast(FP8X4),
+                scales=f_scales[j][:, first_pass * P : end_pass * P],
+                in_=f_grouped[j][:, first_pass * K_PASS : end_pass * K_PASS],
+            )
+
+        def first_sum(h):
+            cols = slice(h * HALF, (h + 1) * HALF)
+            nc.vector.scalar_tensor_tensor(
+                out=x1[:, cols], in0=y[0][h][:], scalar=coeff_f32[:, 0:1], in1=x_sb[:, cols],
+                op0=MULT, op1=ADD,
+            )
+            x1_by_k = x1[:].rearrange("s (g u p e) -> s g u e p", g=PASSES, u=2, p=P, e=2)
+            x1_t = psum.tile([P, PACK, P], F32, name="x1_t_%d" % h)
+            for u in range(2):
+                for e in range(2):
+                    nc.tensor.transpose(x1_t[:, 2 * u + e, :], x1_by_k[:, h, u, e, :], ident[:])
+            nc.scalar.copy(
+                out=f_grouped[1][:, h * K_PASS : (h + 1) * K_PASS].rearrange("p (s t) -> p s t", t=PACK),
+                in_=x1_t[:].rearrange("p t s -> p s t"),
+            )
+            quantise_features(1, h, h + 1)
+
+        def second_sum(h):
+            cols = slice(h * HALF, (h + 1) * HALF)
+            nc.vector.scalar_tensor_tensor(
+                out=result[:, cols], in0=y[1][h][:], scalar=coeff_f32[:, 1:2], in1=x1[:, cols],
+                op0=MULT, op1=ADD,
+            )
+            nc.sync.dma_start(out=out[:, cols], in_=result[:, cols])
+
+        x_words = x_sb[:].bitcast(F32)
+        x_t = psum.tile([P, PASSES * 2, P], F32)
+        for b in range(PASSES * 2):
+            nc.tensor.transpose(x_t[:, b, :], x_words[:, b * P : (b + 1) * P], ident[:])
+        nc.scalar.copy(
+            out=f_grouped[0][:].bitcast(F32).rearrange("p (g s u) -> p g s u", g=PASSES, u=2),
+            in_=x_t[:].rearrange("p (g u) s -> p g s u", u=2),
+        )
+        quantise_features(0, 0, PASSES)
+
+        chunks = [(j, g, h) for j in range(STEPS) for g in range(PASSES) for h in range(HALVES)]
+
+        def finish(j, g, h, grouped):
+            quantise_and_multiply(j, g, h, grouped)
+            if g == PASSES - 1 and j == 0:
+                first_sum(h)
+            if g == PASSES - 1 and j == 1:
+                second_sum(h)
+
+        regrouped = [regroup(*chunks[0])]
+        for i in range(1, len(chunks)):
+            regrouped.append(regroup(*chunks[i]))
+            finish(*chunks[i - 1], regrouped[i - 1])
+        finish(*chunks[-1], regrouped[-1])

@@ -23,6 +23,11 @@ RUN = 4
 
 SCALAR_COLS = 288
 
+QUANTISE_LAG = 1
+SUM_LAG = 2
+COPY_LAG = 3
+FEATURES_LAG = 4
+
 FLOPS = 2 * STEPS * P * D * D
 
 
@@ -32,6 +37,7 @@ def tile_precomputedmetanet_pa_s_kernel(tc, transformed, coeff, task_mats, out):
         keep = ctx.enter_context(tc.tile_pool(name="keep", bufs=1))
         stage = ctx.enter_context(tc.tile_pool(name="stage", bufs=3))
         psum = ctx.enter_context(tc.psum_pool(name="psum", bufs=1))
+        ctx.enter_context(tc.manual_schedule())
 
         x_sb = keep.tile([P, D], BF16)
         nc.scalar.dma_start(out=x_sb[:], in_=transformed)
@@ -60,7 +66,7 @@ def tile_precomputedmetanet_pa_s_kernel(tc, transformed, coeff, task_mats, out):
         ident = keep.tile([P, P], F32)
         make_identity(nc, ident[:])
         coeff_f32 = keep.tile([P, STEPS], F32)
-        nc.vector.tensor_copy(out=coeff_f32[:], in_=coeff_bf[:])
+        nc.gpsimd.tensor_copy(out=coeff_f32[:], in_=coeff_bf[:])
 
         m_codes = [
             [keep.tile([P, D], U32, align_bytes=64, name="m_codes_%d_%d" % (j, g)) for g in range(PASSES)]
@@ -81,36 +87,41 @@ def tile_precomputedmetanet_pa_s_kernel(tc, transformed, coeff, task_mats, out):
             for j in range(STEPS)
         ]
 
+        x1_t = [psum.tile([P, PACK, P], F32, name="x1_t_%d" % h) for h in range(HALVES)]
+        grouped = {}
+
         def regroup(j, g, h):
-            grouped = stage.tile([P, HALF, PACK], BF16, align_bytes=64)
+            tile_ = stage.tile([P, HALF, PACK], BF16, align_bytes=64, name="grouped")
             first = h * HALF
             nc.scalar.copy(
-                out=grouped[:, :SCALAR_COLS, :].rearrange("p (c i) t -> p c t i", i=RUN),
+                out=tile_[:, :SCALAR_COLS, :].rearrange("p (c i) t -> p c t i", i=RUN),
                 in_=raw[j][g][:, :, first : first + SCALAR_COLS].rearrange("p t (c i) -> p c t i", i=RUN),
             )
             nc.vector.tensor_copy(
-                out=grouped[:, SCALAR_COLS:, :].rearrange("p (c i) t -> p c t i", i=RUN),
+                out=tile_[:, SCALAR_COLS:, :].rearrange("p (c i) t -> p c t i", i=RUN),
                 in_=raw[j][g][:, :, first + SCALAR_COLS : first + HALF].rearrange("p t (c i) -> p c t i", i=RUN),
             )
-            return grouped
+            grouped[(j, g, h)] = tile_
 
-        def quantise_and_multiply(j, g, h, grouped):
+        def quantise_and_multiply(j, g, h):
             cols = slice(h * HALF, (h + 1) * HALF)
-            samples = slice(g * P, (g + 1) * P)
             nc.vector.quantize_mx(
                 out=m_codes[j][g][:, cols].bitcast(FP8X4),
                 scales=m_scales[j][g][:, cols],
-                in_=grouped[:].rearrange("p c t -> p (c t)"),
+                in_=grouped[(j, g, h)][:].rearrange("p c t -> p (c t)"),
             )
-            nc.tensor.matmul_mx(
-                out=y[j][h][:],
-                lhsT=f_codes[j][:, samples].bitcast(FP8X4),
-                lhsT_scale=f_scales[j][:, samples],
-                rhs=m_codes[j][g][:, cols].bitcast(FP8X4),
-                rhs_scale=m_scales[j][g][:, cols],
-                start=(g == 0),
-                stop=(g == PASSES - 1),
-            )
+            if g == PASSES - 1:
+                for c in range(PASSES):
+                    samples = slice(c * P, (c + 1) * P)
+                    nc.tensor.matmul_mx(
+                        out=y[j][h][:],
+                        lhsT=f_codes[j][:, samples].bitcast(FP8X4),
+                        lhsT_scale=f_scales[j][:, samples],
+                        rhs=m_codes[j][c][:, cols].bitcast(FP8X4),
+                        rhs_scale=m_scales[j][c][:, cols],
+                        start=(c == 0),
+                        stop=(c == PASSES - 1),
+                    )
 
         def quantise_features(j, first_pass, end_pass):
             nc.vector.quantize_mx(
@@ -119,30 +130,34 @@ def tile_precomputedmetanet_pa_s_kernel(tc, transformed, coeff, task_mats, out):
                 in_=f_grouped[j][:, first_pass * K_PASS : end_pass * K_PASS],
             )
 
-        def first_sum(h):
+        def add_residual(j, g, h):
             cols = slice(h * HALF, (h + 1) * HALF)
-            nc.vector.scalar_tensor_tensor(
-                out=x1[:, cols], in0=y[0][h][:], scalar=coeff_f32[:, 0:1], in1=x_sb[:, cols],
-                op0=MULT, op1=ADD,
-            )
-            x1_by_k = x1[:].rearrange("s (g u p e) -> s g u e p", g=PASSES, u=2, p=P, e=2)
-            x1_t = psum.tile([P, PACK, P], F32, name="x1_t_%d" % h)
-            for u in range(2):
-                for e in range(2):
-                    nc.tensor.transpose(x1_t[:, 2 * u + e, :], x1_by_k[:, h, u, e, :], ident[:])
-            nc.scalar.copy(
-                out=f_grouped[1][:, h * K_PASS : (h + 1) * K_PASS].rearrange("p (s t) -> p s t", t=PACK),
-                in_=x1_t[:].rearrange("p t s -> p s t"),
-            )
-            quantise_features(1, h, h + 1)
+            if g == PASSES - 1 and j == 0:
+                nc.vector.scalar_tensor_tensor(
+                    out=x1[:, cols], in0=y[0][h][:], scalar=coeff_f32[:, 0:1], in1=x_sb[:, cols],
+                    op0=MULT, op1=ADD,
+                )
+                x1_by_k = x1[:].rearrange("s (g u p e) -> s g u e p", g=PASSES, u=2, p=P, e=2)
+                for u in range(2):
+                    for e in range(2):
+                        nc.tensor.transpose(x1_t[h][:, 2 * u + e, :], x1_by_k[:, h, u, e, :], ident[:])
+            if g == PASSES - 1 and j == 1:
+                nc.vector.scalar_tensor_tensor(
+                    out=result[:, cols], in0=y[1][h][:], scalar=coeff_f32[:, 1:2], in1=x1[:, cols],
+                    op0=MULT, op1=ADD,
+                )
+                nc.sync.dma_start(out=out[:, cols], in_=result[:, cols])
 
-        def second_sum(h):
-            cols = slice(h * HALF, (h + 1) * HALF)
-            nc.vector.scalar_tensor_tensor(
-                out=result[:, cols], in0=y[1][h][:], scalar=coeff_f32[:, 1:2], in1=x1[:, cols],
-                op0=MULT, op1=ADD,
-            )
-            nc.sync.dma_start(out=out[:, cols], in_=result[:, cols])
+        def round_x1(j, g, h):
+            if g == PASSES - 1 and j == 0:
+                nc.scalar.copy(
+                    out=f_grouped[1][:, h * K_PASS : (h + 1) * K_PASS].rearrange("p (s t) -> p s t", t=PACK),
+                    in_=x1_t[h][:].rearrange("p t s -> p s t"),
+                )
+
+        def quantise_x1(j, g, h):
+            if g == PASSES - 1 and j == 0:
+                quantise_features(1, h, h + 1)
 
         x_words = x_sb[:].bitcast(F32)
         x_t = psum.tile([P, PASSES * 2, P], F32)
@@ -156,15 +171,13 @@ def tile_precomputedmetanet_pa_s_kernel(tc, transformed, coeff, task_mats, out):
 
         chunks = [(j, g, h) for j in range(STEPS) for g in range(PASSES) for h in range(HALVES)]
 
-        def finish(j, g, h, grouped):
-            quantise_and_multiply(j, g, h, grouped)
-            if g == PASSES - 1 and j == 0:
-                first_sum(h)
-            if g == PASSES - 1 and j == 1:
-                second_sum(h)
+        def at(stage_of_pipeline, i):
+            if 0 <= i < len(chunks):
+                stage_of_pipeline(*chunks[i])
 
-        regrouped = [regroup(*chunks[0])]
-        for i in range(1, len(chunks)):
-            regrouped.append(regroup(*chunks[i]))
-            finish(*chunks[i - 1], regrouped[i - 1])
-        finish(*chunks[-1], regrouped[-1])
+        for i in range(len(chunks) + FEATURES_LAG):
+            at(regroup, i)
+            at(quantise_x1, i - FEATURES_LAG)
+            at(quantise_and_multiply, i - QUANTISE_LAG)
+            at(add_residual, i - SUM_LAG)
+            at(round_x1, i - COPY_LAG)

@@ -49,19 +49,14 @@ def tile_precomputedmetanet_pa_s_kernel(tc, transformed, coeff, task_mats, out):
             for j in range(STEPS)
         ]
         by_k = task_mats.rearrange("j (g u p e) n -> j g p u e n", g=PASSES, u=2, p=P, e=2)
-        for h in range(HALVES):
-            for u in range(2):
-                nc.sync.dma_start(
-                    out=raw[0][0][:, 2 * u : 2 * u + 2, h * HALF : (h + 1) * HALF],
-                    in_=by_k[0, 0, :, u, :, h * HALF : (h + 1) * HALF],
-                )
         for j in range(STEPS):
             for g in range(PASSES):
-                if (j, g) != (0, 0):
-                    nc.sync.dma_start(
-                        out=raw[j][g][:].rearrange("p (u e) n -> p u e n", u=2),
-                        in_=by_k[j, g],
-                    )
+                for h in range(HALVES):
+                    for u in range(2):
+                        nc.sync.dma_start(
+                            out=raw[j][g][:, 2 * u : 2 * u + 2, h * HALF : (h + 1) * HALF],
+                            in_=by_k[j, g, :, u, :, h * HALF : (h + 1) * HALF],
+                        )
 
         ident = keep.tile([P, P], F32)
         make_identity(nc, ident[:])

@@ -21,7 +21,7 @@ HALF = 512
 HALVES = D // HALF
 RUN = 4
 
-SCALAR_COLS = 288
+SCALAR_COLS = 256
 
 QUANTISE_LAG = 1
 SUM_LAG = 2
@@ -49,14 +49,19 @@ def tile_precomputedmetanet_pa_s_kernel(tc, transformed, coeff, task_mats, out):
             for j in range(STEPS)
         ]
         by_k = task_mats.rearrange("j (g u p e) n -> j g p u e n", g=PASSES, u=2, p=P, e=2)
+        for h in range(HALVES):
+            for u in range(2):
+                nc.sync.dma_start(
+                    out=raw[0][0][:, 2 * u : 2 * u + 2, h * HALF : (h + 1) * HALF],
+                    in_=by_k[0, 0, :, u, :, h * HALF : (h + 1) * HALF],
+                )
         for j in range(STEPS):
             for g in range(PASSES):
-                for h in range(HALVES):
-                    for u in range(2):
-                        nc.sync.dma_start(
-                            out=raw[j][g][:, 2 * u : 2 * u + 2, h * HALF : (h + 1) * HALF],
-                            in_=by_k[j, g, :, u, :, h * HALF : (h + 1) * HALF],
-                        )
+                if (j, g) != (0, 0):
+                    nc.sync.dma_start(
+                        out=raw[j][g][:].rearrange("p (u e) n -> p u e n", u=2),
+                        in_=by_k[j, g],
+                    )
 
         ident = keep.tile([P, P], F32)
         make_identity(nc, ident[:])

from contextlib import ExitStack

import concourse.mybir as mybir
from concourse.masks import make_identity

F32 = mybir.dt.float32
BF16 = mybir.dt.bfloat16
U32 = mybir.dt.uint32
U8 = mybir.dt.uint8
FP8X4 = mybir.dt.float8_e4m3fn_x4
MULT = mybir.AluOpType.mult
ADD = mybir.AluOpType.add

P = 128
PACK = 4
K_PASS = P * PACK
D = 1024
STEPS = 2
PASSES = D // K_PASS
HALF = 512
HALVES = D // HALF
RUN = 4

SCALAR_COLS = 256

QUANTISE_LAG = 1
SUM_LAG = 2
COPY_LAG = 3
FEATURES_LAG = 4

FLOPS = 2 * STEPS * P * D * D


def tile_precomputedmetanet_pa_s_kernel(tc, transformed, coeff, task_mats, out):
    nc = tc.nc
    with ExitStack() as ctx:
        keep = ctx.enter_context(tc.tile_pool(name="keep", bufs=1))
        stage = ctx.enter_context(tc.tile_pool(name="stage", bufs=3))
        psum = ctx.enter_context(tc.psum_pool(name="psum", bufs=1))
        ctx.enter_context(tc.manual_schedule())

        x_sb = keep.tile([P, D], BF16)
        nc.scalar.dma_start(out=x_sb[:], in_=transformed)
        coeff_bf = keep.tile([P, STEPS], BF16)
        nc.scalar.dma_start(out=coeff_bf[:], in_=coeff)

        raw = [
            [keep.tile([P, PACK, D], BF16, name="raw_%d_%d" % (j, g)) for g in range(PASSES)]
            for j in range(STEPS)
        ]
        by_k = task_mats.rearrange("j (g u p e) n -> j g p u e n", g=PASSES, u=2, p=P, e=2)
        for h in range(HALVES):
            for u in range(2):
                nc.sync.dma_start(
                    out=raw[0][0][:, 2 * u : 2 * u + 2, h * HALF : (h + 1) * HALF],
                    in_=by_k[0, 0, :, u, :, h * HALF : (h + 1) * HALF],
                )
        for j in range(STEPS):
            for g in range(PASSES):
                if (j, g) != (0, 0):
                    nc.sync.dma_start(
                        out=raw[j][g][:].rearrange("p (u e) n -> p u e n", u=2),
                        in_=by_k[j, g],
                    )

        ident = keep.tile([P, P], F32)
        make_identity(nc, ident[:])
        coeff_f32 = keep.tile([P, STEPS], F32)
        nc.gpsimd.tensor_copy(out=coeff_f32[:], in_=coeff_bf[:])

        m_codes = [
            [keep.tile([P, D], U32, align_bytes=64, name="m_codes_%d_%d" % (j, g)) for g in range(PASSES)]
            for j in range(STEPS)
        ]
        m_scales = [
            [keep.tile([P, D], U8, align_bytes=64, name="m_scales_%d_%d" % (j, g)) for g in range(PASSES)]
            for j in range(STEPS)
        ]
        f_grouped = [keep.tile([P, PASSES * P * PACK], BF16, align_bytes=64, name="f_grouped_%d" % j) for j in range(STEPS)]
        f_codes = [keep.tile([P, PASSES * P], U32, align_bytes=64, name="f_codes_%d" % j) for j in range(STEPS)]
        f_scales = [keep.tile([P, PASSES * P], U8, align_bytes=64, name="f_scales_%d" % j) for j in range(STEPS)]

        x1 = keep.tile([P, D], F32)
        result = keep.tile([P, D], F32)
        y = [
            [psum.tile([P, HALF], F32, name="y_%d_%d" % (j, h)) for h in range(HALVES)]
            for j in range(STEPS)
        ]

        x1_t = [psum.tile([P, PACK, P], F32, name="x1_t_%d" % h) for h in range(HALVES)]
        grouped = {}

        def regroup(j, g, h):
            tile_ = stage.tile([P, HALF, PACK], BF16, align_bytes=64, name="grouped")
            first = h * HALF
            nc.scalar.copy(
                out=tile_[:, :SCALAR_COLS, :].rearrange("p (c i) t -> p c t i", i=RUN),
                in_=raw[j][g][:, :, first : first + SCALAR_COLS].rearrange("p t (c i) -> p c t i", i=RUN),
            )
            nc.vector.tensor_copy(
                out=tile_[:, SCALAR_COLS:, :].rearrange("p (c i) t -> p c t i", i=RUN),
                in_=raw[j][g][:, :, first + SCALAR_COLS : first + HALF].rearrange("p t (c i) -> p c t i", i=RUN),
            )
            grouped[(j, g, h)] = tile_

        def quantise_and_multiply(j, g, h):
            cols = slice(h * HALF, (h + 1) * HALF)
            nc.vector.quantize_mx(
                out=m_codes[j][g][:, cols].bitcast(FP8X4),
                scales=m_scales[j][g][:, cols],
                in_=grouped[(j, g, h)][:].rearrange("p c t -> p (c t)"),
            )
            if g == PASSES - 1:
                for c in range(PASSES):
                    samples = slice(c * P, (c + 1) * P)
                    nc.tensor.matmul_mx(
                        out=y[j][h][:],
                        lhsT=f_codes[j][:, samples].bitcast(FP8X4),
                        lhsT_scale=f_scales[j][:, samples],
                        rhs=m_codes[j][c][:, cols].bitcast(FP8X4),
                        rhs_scale=m_scales[j][c][:, cols],
                        start=(c == 0),
                        stop=(c == PASSES - 1),
                    )

        def quantise_features(j, first_pass, end_pass):
            nc.vector.quantize_mx(
                out=f_codes[j][:, first_pass * P : end_pass * P].bitcast(FP8X4),
                scales=f_scales[j][:, first_pass * P : end_pass * P],
                in_=f_grouped[j][:, first_pass * K_PASS : end_pass * K_PASS],
            )

        def add_residual(j, g, h):
            cols = slice(h * HALF, (h + 1) * HALF)
            if g == PASSES - 1 and j == 0:
                nc.vector.scalar_tensor_tensor(
                    out=x1[:, cols], in0=y[0][h][:], scalar=coeff_f32[:, 0:1], in1=x_sb[:, cols],
                    op0=MULT, op1=ADD,
                )
                x1_by_k = x1[:].rearrange("s (g u p e) -> s g u e p", g=PASSES, u=2, p=P, e=2)
                for u in range(2):
                    for e in range(2):
                        nc.tensor.transpose(x1_t[h][:, 2 * u + e, :], x1_by_k[:, h, u, e, :], ident[:])
            if g == PASSES - 1 and j == 1:
                nc.vector.scalar_tensor_tensor(
                    out=result[:, cols], in0=y[1][h][:], scalar=coeff_f32[:, 1:2], in1=x1[:, cols],
                    op0=MULT, op1=ADD,
                )
                nc.sync.dma_start(out=out[:, cols], in_=result[:, cols])

        def round_x1(j, g, h):
            if g == PASSES - 1 and j == 0:
                nc.scalar.copy(
                    out=f_grouped[1][:, h * K_PASS : (h + 1) * K_PASS].rearrange("p (s t) -> p s t", t=PACK),
                    in_=x1_t[h][:].rearrange("p t s -> p s t"),
                )

        def quantise_x1(j, g, h):
            if g == PASSES - 1 and j == 0:
                quantise_features(1, h, h + 1)

        x_words = x_sb[:].bitcast(F32)
        x_t = psum.tile([P, PASSES * 2, P], F32)
        for b in range(PASSES * 2):
            nc.tensor.transpose(x_t[:, b, :], x_words[:, b * P : (b + 1) * P], ident[:])
        nc.scalar.copy(
            out=f_grouped[0][:].bitcast(F32).rearrange("p (g s u) -> p g s u", g=PASSES, u=2),
            in_=x_t[:].rearrange("p (g u) s -> p g s u", u=2),
        )
        quantise_features(0, 0, PASSES)

        chunks = [(j, g, h) for j in range(STEPS) for g in range(PASSES) for h in range(HALVES)]

        def at(stage_of_pipeline, i):
            if 0 <= i < len(chunks):
                stage_of_pipeline(*chunks[i])

        for i in range(len(chunks) + FEATURES_LAG):
            at(regroup, i)
            at(quantise_x1, i - FEATURES_LAG)
            at(quantise_and_multiply, i - QUANTISE_LAG)
            at(add_residual, i - SUM_LAG)
            at(round_x1, i - COPY_LAG)
